import numpy as np
import ml_dtypes


def mxq(x, axis, fmt="e4m3"):
    dtype, down = {"e4m3": (ml_dtypes.float8_e4m3fn, 7), "e5m2": (ml_dtypes.float8_e5m2, 14)}[fmt]
    v = np.moveaxis(np.asarray(x, np.float32).astype(ml_dtypes.bfloat16).astype(np.float64), axis, -1)
    blocks = v.reshape(v.shape[:-1] + (-1, 32))
    amax = np.abs(blocks).max(-1, keepdims=True)
    byte = np.maximum(np.where(amax > 0, np.frexp(amax)[1] - 1 + 127, 0) - down, 1)
    scale = np.exp2(byte - 127.0)
    codes = (blocks / scale).astype(np.float32).astype(dtype).astype(np.float64)
    return np.moveaxis((codes * scale).reshape(v.shape), -1, axis)


WIDE = False


def mx_kscale(k):
    if not WIDE:
        return np.ones(k)
    levels = np.array([10, -10, 5, -5, 0])
    a = np.random.permutation(np.resize(levels, k // 512 * 4)).reshape(k // 512, 4)
    idx = np.arange(k)
    return np.exp2(a[idx // 512, idx % 128 // 32])


BF16 = ml_dtypes.bfloat16


def bf(x):
    return np.asarray(x, np.float32).astype(BF16)


def f64(x):
    return np.asarray(x).astype(np.float64)


B, N, D = 16, 256, 1024
P0 = 0.2


def setup_inputs():
    s = mx_kscale(D)
    g = 0.4 + 1.2 * np.random.random_sample((B, 1, N))
    bound = np.sqrt(6.0 / (D + D))
    return {"embedding": bf(np.random.standard_normal((B, D, N)) * g * np.sqrt(P0) / D ** 0.25 * s[None, :, None]),
            "heatm": bf(np.random.standard_normal((B, D, N))),
            "W_b": bf(np.random.uniform(-bound, bound, (D, D)) / s[:, None] / s[None, :])}


def reference(embedding, heatm, W_b):
    eq = mxq(f64(embedding), 1, "e4m3")
    t = np.swapaxes(eq, 1, 2) @ mxq(f64(W_b), 0, "e4m3")
    C = np.tanh(mxq(t, 2, "e4m3") @ eq)
    max_cow = np.max(C, axis=-1, keepdims=True)
    e = np.exp(max_cow - np.max(max_cow, axis=1, keepdims=True))
    return e / np.sum(e, axis=1, keepdims=True)

@@ -1,0 +1,219 @@
+from contextlib import ExitStack
+
+import concourse.mybir as mybir
+from concourse.masks import make_identity
+
+FLOPS = 2 * 4096 * 1024 * 1024 + 16 * 2 * 256 * 256 * 1024
+BYTES = 16 * 1024 * 256 * 2 + 1024 * 1024 * 2 + 16 * 256 * 4
+
+BF16 = mybir.dt.bfloat16
+F32 = mybir.dt.float32
+U32 = mybir.dt.uint32
+U8 = mybir.dt.uint8
+FP8X4 = mybir.dt.float8_e4m3fn_x4
+ACT = mybir.ActivationFunctionType
+ALU = mybir.AluOpType
+AX = mybir.AxisListType
+
+P = 128
+PACK = 4
+B = 16
+N = 256
+D = 1024
+KP = 2
+W_SPLIT = 84
+
+
+def tile_parallelcoattention_t_kernel(tc, embedding, heatm, W_b, out):
+    nc = tc.nc
+    with ExitStack() as ctx:
+        keep = ctx.enter_context(tc.tile_pool(name="keep", bufs=1))
+        stage = ctx.enter_context(tc.tile_pool(name="stage", bufs=3))
+        psum = ctx.enter_context(tc.psum_pool(name="psum", bufs=1))
+        ctx.enter_context(tc.manual_schedule())
+
+        warm = keep.tile([P, 1], F32, name="warm")
+        nc.vector.memset(warm[:], 0.0)
+        warm2 = keep.tile([P, 1], F32, name="warm2")
+        nc.scalar.activation(out=warm2[:], in_=warm[:], func=ACT.Tanh)
+        rowmax = keep.tile([P, 2, P], F32, name="rowmax")
+        nc.vector.memset(rowmax[:], 0.0)
+        ident = keep.tile([P, P], F32, name="ident")
+        make_identity(nc, ident[:])
+
+        w_view = W_b.rearrange("(c p k) w -> c p k w", c=KP, p=P, k=PACK)
+        w_raw = {}
+        e_raw = {}
+
+        def load_w(ck, co):
+            t = keep.tile([P, PACK, 512], BF16, name="wraw%d%d" % (ck, co))
+            nc.sync.dma_start(out=t[:], in_=w_view[ck][:, :, co * 512 : (co + 1) * 512])
+            w_raw[(ck, co)] = t
+
+        def load_e(b):
+            t = keep.tile([P, KP, PACK, N], BF16, name="eraw%d" % b)
+            nc.sync.dma_start(
+                out=t[:], in_=embedding[b].rearrange("(c p k) n -> p c k n", c=KP, p=P, k=PACK)
+            )
+            e_raw[b] = t
+
+        load_w(0, 0)
+        load_w(1, 0)
+        load_e(0)
+        load_w(0, 1)
+        load_w(1, 1)
+        for b in range(1, B):
+            load_e(b)
+
+        w_codes = {}
+        w_scales = {}
+        w_grouped = {}
+
+        def regroup_w(ck, co):
+            g = keep.tile([P, PACK, P, PACK], BF16, name="wg%d%d" % (ck, co), align_bytes=64)
+            src = w_raw[(ck, co)][:].rearrange("p k (q j) -> p j q k", j=PACK)
+            nc.vector.tensor_copy(out=g[:, :, 0:W_SPLIT, :], in_=src[:, :, 0:W_SPLIT, :])
+            nc.scalar.copy(out=g[:, :, W_SPLIT:P, :], in_=src[:, :, W_SPLIT:P, :])
+            w_grouped[(ck, co)] = g
+
+        def quantise_w(ck, co):
+            c = keep.tile([P, 512], U32, name="wc%d%d" % (ck, co), align_bytes=64)
+            s = keep.tile([P, 512], U8, name="ws%d%d" % (ck, co), align_bytes=64)
+            nc.vector.quantize_mx(
+                out=c[:].bitcast(FP8X4),
+                scales=s[:],
+                in_=w_grouped[(ck, co)][:].rearrange("p j q k -> p (j q k)"),
+            )
+            w_codes[(ck, co)] = c
+            w_scales[(ck, co)] = s
+
+        e_grouped = {}
+        e_codes = {}
+        e_scales = {}
+
+        def regroup_part(eng_copy, g, raw, c, n0, n1):
+            eng_copy(
+                out=g[:, c, n0:n1, :].rearrange("p (g i) t -> p g t i", i=4),
+                in_=raw[:, c, :, n0:n1].rearrange("p t (g i) -> p g t i", i=4),
+            )
+
+        def regroup_e(b):
+            g = stage.tile([P, KP, N, PACK], BF16, name="eg", align_bytes=64)
+            raw = e_raw[b]
+            regroup_part(nc.scalar.copy, g, raw, 1, 128, N)
+            regroup_part(nc.vector.tensor_copy, g, raw, 0, 0, N)
+            regroup_part(nc.vector.tensor_copy, g, raw, 1, 0, 128)
+            e_grouped[b] = g
+
+        def quantise_e(b):
+            c = keep.tile([P, KP, N], U32, name="ec%d" % b, align_bytes=64)
+            s = keep.tile([P, KP, N], U8, name="es%d" % b, align_bytes=64)
+            nc.vector.quantize_mx(
+                out=c[:].rearrange("p c n -> p (c n)").bitcast(FP8X4),
+                scales=s[:].rearrange("p c n -> p (c n)"),
+                in_=e_grouped[b][:].rearrange("p c n k -> p (c n k)"),
+            )
+            e_codes[b] = c
+            e_scales[b] = s
+
+        t_grouped = {}
+        t_codes = {}
+        t_scales = {}
+
+        def mm1(b):
+            g = stage.tile([P, KP, N, PACK], BF16, name="tg", align_bytes=64)
+            t_grouped[b] = g
+            for co in range(KP):
+                for nh in range(2):
+                    cols = slice(nh * P, (nh + 1) * P)
+                    bank = psum.tile([P, PACK, P], F32, name="tb", bufs=6)
+                    for j in range(PACK):
+                        wcols = slice(j * P, (j + 1) * P)
+                        for ck in range(KP):
+                            nc.tensor.matmul_mx(
+                                out=bank[:, j, :],
+                                lhsT=w_codes[(ck, co)][:, wcols].bitcast(FP8X4),
+                                lhsT_scale=w_scales[(ck, co)][:, wcols],
+                                rhs=e_codes[b][:, ck, cols].bitcast(FP8X4),
+                                rhs_scale=e_scales[b][:, ck, cols],
+                                start=(ck == 0),
+                                stop=(ck == KP - 1),
+                            )
+                    nc.scalar.copy(out=g[:, co, cols, :], in_=bank[:].rearrange("p j n -> p n j"))
+
+        def quantise_t(b):
+            c = stage.tile([P, KP, N], U32, name="tc", align_bytes=64)
+            s = stage.tile([P, KP, N], U8, name="ts", align_bytes=64)
+            nc.vector.quantize_mx(
+                out=c[:].rearrange("p c n -> p (c n)").bitcast(FP8X4),
+                scales=s[:].rearrange("p c n -> p (c n)"),
+                in_=t_grouped[b][:].rearrange("p c n k -> p (c n k)"),
+            )
+            t_codes[b] = c
+            t_scales[b] = s
+
+        c_banks = {}
+
+        def mm2(b):
+            bank = psum.tile([P, 2, N], F32, name="cb", bufs=2)
+            for nt in range(2):
+                rows = slice(nt * P, (nt + 1) * P)
+                for c in range(KP):
+                    nc.tensor.matmul_mx(
+                        out=bank[:, nt, :],
+                        lhsT=t_codes[b][:, c, rows].bitcast(FP8X4),
+                        lhsT_scale=t_scales[b][:, c, rows],
+                        rhs=e_codes[b][:, c, :].bitcast(FP8X4),
+                        rhs_scale=e_scales[b][:, c, :],
+                        start=(c == 0),
+                        stop=(c == KP - 1),
+                    )
+            c_banks[b] = bank
+
+        def row_max(b):
+            nc.vector.tensor_reduce(out=rowmax[:, :, b], in_=c_banks[b][:], axis=AX.X, op=ALU.max)
+
+        regroup_w(0, 0)
+        regroup_w(1, 0)
+        quantise_w(0, 0)
+        regroup_e(0)
+        quantise_w(1, 0)
+        regroup_w(0, 1)
+        quantise_e(0)
+        regroup_w(1, 1)
+        quantise_w(0, 1)
+        regroup_e(1)
+        quantise_w(1, 1)
+        regroup_e(2)
+        quantise_e(1)
+        mm1(0)
+        for i in range(B):
+            if i >= 1:
+                row_max(i - 1)
+            quantise_t(i)
+            if i + 3 < B:
+                regroup_e(i + 3)
+            if i + 2 < B:
+                quantise_e(i + 2)
+            if i + 1 < B:
+                mm1(i + 1)
+            mm2(i)
+        row_max(B - 1)
+
+        tp = psum.tile([P, 2, P], F32, name="cb", bufs=2)
+        for nt in range(2):
+            nc.tensor.transpose(tp[:, nt, :], rowmax[:, nt, :], ident[:])
+        th = keep.tile([P, N], F32, name="th")
+        nc.scalar.activation(out=th[:], in_=tp[:].rearrange("p t n -> p (t n)"), func=ACT.Tanh)
+        negmax = keep.tile([P, 1], F32, name="negmax")
+        nc.vector.tensor_reduce(out=negmax[:], in_=th[:], axis=AX.X, op=ALU.max, negate=True)
+        ex = keep.tile([P, N], F32, name="ex")
+        esum = keep.tile([P, 1], F32, name="esum")
+        nc.scalar.activation(
+            out=ex[:], in_=th[:], func=ACT.Exp, bias=negmax[:, 0:1], scale=1.0, accum_out=esum[:]
+        )
+        rsum = keep.tile([P, 1], F32, name="rsum")
+        nc.vector.reciprocal(out=rsum[:], in_=esum[:])
+        res = keep.tile([P, N], F32, name="res")
+        nc.vector.tensor_scalar_mul(out=res[:], in0=ex[:], scalar1=rsum[:, 0:1])
+        nc.sync.dma_start(out=out.rearrange("b n o -> b (n o)"), in_=res[0:B, :])

@@ -19,9 +19,15 @@ P = 128
 PACK = 4
 B = 16
 N = 256
-D = 1024
 KP = 2
-W_SPLIT = 84
+
+
+def scalar_share(b):
+    if b < 2:
+        return 1024
+    if b < 4:
+        return 0
+    return 512
 
 
 def tile_parallelcoattention_t_kernel(tc, embedding, heatm, W_b, out):
@@ -29,7 +35,7 @@ def tile_parallelcoattention_t_kernel(tc, embedding, heatm, W_b, out):
     with ExitStack() as ctx:
         keep = ctx.enter_context(tc.tile_pool(name="keep", bufs=1))
         stage = ctx.enter_context(tc.tile_pool(name="stage", bufs=3))
-        psum = ctx.enter_context(tc.psum_pool(name="psum", bufs=1))
+        psum = ctx.enter_context(tc.psum_pool(name="psum", bufs=8))
         ctx.enter_context(tc.manual_schedule())
 
         warm = keep.tile([P, 1], F32, name="warm")
@@ -60,50 +66,63 @@ def tile_parallelcoattention_t_kernel(tc, embedding, heatm, W_b, out):
         load_w(0, 0)
         load_w(1, 0)
         load_e(0)
+        load_e(1)
         load_w(0, 1)
         load_w(1, 1)
-        for b in range(1, B):
+        for b in range(2, B):
             load_e(b)
 
+        w_grouped = {}
         w_codes = {}
         w_scales = {}
-        w_grouped = {}
+        for co in range(KP):
+            for jp in range(2):
+                w_grouped[(co, jp)] = keep.tile(
+                    [P, 2, KP, P, PACK], BF16, name="wg%d%d" % (co, jp), align_bytes=64
+                )
 
-        def regroup_w(ck, co):
-            g = keep.tile([P, PACK, P, PACK], BF16, name="wg%d%d" % (ck, co), align_bytes=64)
+        def regroup_w(copy, ck, co, jp):
             src = w_raw[(ck, co)][:].rearrange("p k (q j) -> p j q k", j=PACK)
-            nc.vector.tensor_copy(out=g[:, :, 0:W_SPLIT, :], in_=src[:, :, 0:W_SPLIT, :])
-            nc.scalar.copy(out=g[:, :, W_SPLIT:P, :], in_=src[:, :, W_SPLIT:P, :])
-            w_grouped[(ck, co)] = g
+            copy(out=w_grouped[(co, jp)][:, :, ck, :, :], in_=src[:, 2 * jp : 2 * jp + 2, :, :])
 
-        def quantise_w(ck, co):
-            c = keep.tile([P, 512], U32, name="wc%d%d" % (ck, co), align_bytes=64)
-            s = keep.tile([P, 512], U8, name="ws%d%d" % (ck, co), align_bytes=64)
+        def regroup_w_v(ck, co):
+            regroup_w(nc.vector.tensor_copy, ck, co, 0)
+
+        def regroup_w_s(ck, co):
+            regroup_w(nc.scalar.copy, ck, co, 1)
+
+        def quantise_w(co, j):
+            c = keep.tile([P, KP, P], U32, name="wc%d%d" % (co, j), align_bytes=64)
+            s = keep.tile([P, KP, P], U8, name="ws%d%d" % (co, j), align_bytes=64)
             nc.vector.quantize_mx(
-                out=c[:].bitcast(FP8X4),
-                scales=s[:],
-                in_=w_grouped[(ck, co)][:].rearrange("p j q k -> p (j q k)"),
+                out=c[:].rearrange("p c q -> p (c q)").bitcast(FP8X4),
+                scales=s[:].rearrange("p c q -> p (c q)"),
+                in_=w_grouped[(co, j // 2)][:, j % 2, :, :, :].rearrange("p c q k -> p (c q k)"),
             )
-            w_codes[(ck, co)] = c
-            w_scales[(ck, co)] = s
+            w_codes[(co, j)] = c
+            w_scales[(co, j)] = s
 
         e_grouped = {}
         e_codes = {}
         e_scales = {}
 
-        def regroup_part(eng_copy, g, raw, c, n0, n1):
-            eng_copy(
-                out=g[:, c, n0:n1, :].rearrange("p (g i) t -> p g t i", i=4),
-                in_=raw[:, c, :, n0:n1].rearrange("p t (g i) -> p g t i", i=4),
+        def regroup_part(copy, b, c, n0, n1):
+            copy(
+                out=e_grouped[b][:, c, n0:n1, :].rearrange("p (g i) t -> p g t i", i=4),
+                in_=e_raw[b][:, c, :, n0:n1].rearrange("p t (g i) -> p g t i", i=4),
             )
 
-        def regroup_e(b):
-            g = stage.tile([P, KP, N, PACK], BF16, name="eg", align_bytes=64)
-            raw = e_raw[b]
-            regroup_part(nc.scalar.copy, g, raw, 1, 128, N)
-            regroup_part(nc.vector.tensor_copy, g, raw, 0, 0, N)
-            regroup_part(nc.vector.tensor_copy, g, raw, 1, 0, 128)
-            e_grouped[b] = g
+        def regroup_e_s(b):
+            e_grouped[b] = stage.tile([P, KP, N, PACK], BF16, name="eg", bufs=4, align_bytes=64)
+            share = scalar_share(b)
+            if share > 0:
+                regroup_part(nc.scalar.copy, b, 1, N - share // PACK, N)
+
+        def regroup_e_v(b):
+            share = scalar_share(b)
+            regroup_part(nc.vector.tensor_copy, b, 0, 0, N)
+            if share < 1024:
+                regroup_part(nc.vector.tensor_copy, b, 1, 0, N - share // PACK)
 
         def quantise_e(b):
             c = keep.tile([P, KP, N], U32, name="ec%d" % b, align_bytes=64)
@@ -116,91 +135,176 @@ def tile_parallelcoattention_t_kernel(tc, embedding, heatm, W_b, out):
             e_codes[b] = c
             e_scales[b] = s
 
+        t_banks = {}
         t_grouped = {}
         t_codes = {}
         t_scales = {}
 
-        def mm1(b):
-            g = stage.tile([P, KP, N, PACK], BF16, name="tg", align_bytes=64)
-            t_grouped[b] = g
-            for co in range(KP):
-                for nh in range(2):
-                    cols = slice(nh * P, (nh + 1) * P)
-                    bank = psum.tile([P, PACK, P], F32, name="tb", bufs=6)
-                    for j in range(PACK):
-                        wcols = slice(j * P, (j + 1) * P)
-                        for ck in range(KP):
-                            nc.tensor.matmul_mx(
-                                out=bank[:, j, :],
-                                lhsT=w_codes[(ck, co)][:, wcols].bitcast(FP8X4),
-                                lhsT_scale=w_scales[(ck, co)][:, wcols],
-                                rhs=e_codes[b][:, ck, cols].bitcast(FP8X4),
-                                rhs_scale=e_scales[b][:, ck, cols],
-                                start=(ck == 0),
-                                stop=(ck == KP - 1),
-                            )
-                    nc.scalar.copy(out=g[:, co, cols, :], in_=bank[:].rearrange("p j n -> p n j"))
+        def mm1(b, co, nh, js):
+            if (b, co, nh) not in t_banks:
+                t_banks[(b, co, nh)] = psum.tile([P, PACK, P], F32, name="bank")
+            bank = t_banks[(b, co, nh)]
+            cols = slice(nh * P, (nh + 1) * P)
+            for j in js:
+                for ck in range(KP):
+                    nc.tensor.matmul_mx(
+                        out=bank[:, j, :],
+                        lhsT=w_codes[(co, j)][:, ck, :].bitcast(FP8X4),
+                        lhsT_scale=w_scales[(co, j)][:, ck, :],
+                        rhs=e_codes[b][:, ck, cols].bitcast(FP8X4),
+                        rhs_scale=e_scales[b][:, ck, cols],
+                        start=(ck == 0),
+                        stop=(ck == KP - 1),
+                    )
+
+        def evacuate(b, co, nh):
+            if b == B - 1:
+                if (b, nh) not in t_grouped:
+                    t_grouped[(b, nh)] = keep.tile(
+                        [P, KP, P, PACK], BF16, name="tgl%d" % nh, align_bytes=64
+                    )
+                dst = t_grouped[(b, nh)][:, co, :, :]
+            else:
+                if b not in t_grouped:
+                    t_grouped[b] = stage.tile([P, 2, KP, P, PACK], BF16, name="tg", align_bytes=64)
+                dst = t_grouped[b][:, nh, co, :, :]
+            nc.scalar.copy(out=dst, in_=t_banks[(b, co, nh)][:].rearrange("p j n -> p n j"))
 
         def quantise_t(b):
-            c = stage.tile([P, KP, N], U32, name="tc", align_bytes=64)
-            s = stage.tile([P, KP, N], U8, name="ts", align_bytes=64)
+            c = stage.tile([P, 2, KP, P], U32, name="tc", align_bytes=64)
+            s = stage.tile([P, 2, KP, P], U8, name="ts", align_bytes=64)
+            nc.vector.quantize_mx(
+                out=c[:].rearrange("p h c n -> p (h c n)").bitcast(FP8X4),
+                scales=s[:].rearrange("p h c n -> p (h c n)"),
+                in_=t_grouped[b][:].rearrange("p h c n k -> p (h c n k)"),
+            )
+            for nh in range(2):
+                t_codes[(b, nh)] = c[:, nh, :, :]
+                t_scales[(b, nh)] = s[:, nh, :, :]
+
+        def quantise_t_half(b, nh):
+            c = keep.tile([P, KP, P], U32, name="tcl%d" % nh, align_bytes=64)
+            s = keep.tile([P, KP, P], U8, name="tsl%d" % nh, align_bytes=64)
             nc.vector.quantize_mx(
                 out=c[:].rearrange("p c n -> p (c n)").bitcast(FP8X4),
                 scales=s[:].rearrange("p c n -> p (c n)"),
-                in_=t_grouped[b][:].rearrange("p c n k -> p (c n k)"),
+                in_=t_grouped[(b, nh)][:].rearrange("p c n k -> p (c n k)"),
             )
-            t_codes[b] = c
-            t_scales[b] = s
+            t_codes[(b, nh)] = c[:]
+            t_scales[(b, nh)] = s[:]
 
         c_banks = {}
 
+        def mm2_half(b, nt, dst):
+            for c in range(KP):
+                nc.tensor.matmul_mx(
+                    out=dst,
+                    lhsT=t_codes[(b, nt)][:, c, :].bitcast(FP8X4),
+                    lhsT_scale=t_scales[(b, nt)][:, c, :],
+                    rhs=e_codes[b][:, c, :].bitcast(FP8X4),
+                    rhs_scale=e_scales[b][:, c, :],
+                    start=(c == 0),
+                    stop=(c == KP - 1),
+                )
+
         def mm2(b):
-            bank = psum.tile([P, 2, N], F32, name="cb", bufs=2)
-            for nt in range(2):
-                rows = slice(nt * P, (nt + 1) * P)
-                for c in range(KP):
-                    nc.tensor.matmul_mx(
-                        out=bank[:, nt, :],
-                        lhsT=t_codes[b][:, c, rows].bitcast(FP8X4),
-                        lhsT_scale=t_scales[b][:, c, rows],
-                        rhs=e_codes[b][:, c, :].bitcast(FP8X4),
-                        rhs_scale=e_scales[b][:, c, :],
-                        start=(c == 0),
-                        stop=(c == KP - 1),
-                    )
-            c_banks[b] = bank
+            if b == B - 1:
+                for nt in range(2):
+                    bank = psum.tile([P, N], F32, name="bank")
+                    mm2_half(b, nt, bank[:])
+                    c_banks[(b, nt)] = bank
+            else:
+                bank = psum.tile([P, 2, N], F32, name="bank")
+                for nt in range(2):
+                    mm2_half(b, nt, bank[:, nt, :])
+                c_banks[b] = bank
 
         def row_max(b):
-            nc.vector.tensor_reduce(out=rowmax[:, :, b], in_=c_banks[b][:], axis=AX.X, op=ALU.max)
+            if b == B - 1:
+                for nt in range(2):
+                    nc.vector.tensor_reduce(
+                        out=rowmax[:, nt, b : b + 1], in_=c_banks[(b, nt)][:], axis=AX.X, op=ALU.max
+                    )
+            else:
+                nc.vector.tensor_reduce(
+                    out=rowmax[:, :, b], in_=c_banks[b][:], axis=AX.X, op=ALU.max
+                )
 
-        regroup_w(0, 0)
-        regroup_w(1, 0)
+        all_j = [0, 1, 2, 3]
+        regroup_w_v(0, 0)
+        regroup_w_s(0, 0)
+        regroup_w_v(1, 0)
+        regroup_w_s(1, 0)
         quantise_w(0, 0)
-        regroup_e(0)
-        quantise_w(1, 0)
-        regroup_w(0, 1)
-        quantise_e(0)
-        regroup_w(1, 1)
         quantise_w(0, 1)
-        regroup_e(1)
-        quantise_w(1, 1)
-        regroup_e(2)
+        regroup_e_s(0)
+        regroup_e_v(0)
+        quantise_w(0, 2)
+        quantise_w(0, 3)
+        regroup_e_s(1)
+        regroup_e_v(1)
+        quantise_e(0)
+        regroup_w_v(0, 1)
+        regroup_w_s(0, 1)
         quantise_e(1)
-        mm1(0)
-        for i in range(B):
-            if i >= 1:
-                row_max(i - 1)
-            quantise_t(i)
-            if i + 3 < B:
-                regroup_e(i + 3)
-            if i + 2 < B:
-                quantise_e(i + 2)
-            if i + 1 < B:
-                mm1(i + 1)
-            mm2(i)
-        row_max(B - 1)
+        regroup_w_v(1, 1)
+        regroup_w_s(1, 1)
+        for b in range(2):
+            for nh in range(2):
+                mm1(b, 0, nh, all_j)
+                evacuate(b, 0, nh)
+        quantise_w(1, 0)
+        quantise_w(1, 1)
+        regroup_e_s(2)
+        regroup_e_v(2)
+        quantise_w(1, 2)
+        quantise_w(1, 3)
+        quantise_e(2)
+        regroup_e_s(3)
+        regroup_e_v(3)
+        regroup_e_s(4)
+        regroup_e_v(4)
+        for j in all_j:
+            for b in range(2):
+                for nh in range(2):
+                    mm1(b, 1, nh, [j])
+        for b in range(2):
+            for nh in range(2):
+                evacuate(b, 1, nh)
+        quantise_t(0)
+        quantise_e(3)
+        quantise_t(1)
+        regroup_e_s(5)
+        regroup_e_v(5)
 
-        tp = psum.tile([P, 2, P], F32, name="cb", bufs=2)
+        for i in range(B):
+            if i + 6 < B:
+                regroup_e_s(i + 6)
+            if i + 2 < B - 1:
+                for co in range(KP):
+                    for nh in range(2):
+                        mm1(i + 2, co, nh, all_j)
+                        evacuate(i + 2, co, nh)
+            if i + 2 == B - 1:
+                for nh in range(2):
+                    for co in range(KP):
+                        mm1(i + 2, co, nh, all_j)
+                        evacuate(i + 2, co, nh)
+            mm2(i)
+            if i + 2 == B - 1:
+                quantise_t_half(B - 1, 0)
+                row_max(i)
+                quantise_t_half(B - 1, 1)
+            else:
+                row_max(i)
+                if i + 2 < B:
+                    quantise_t(i + 2)
+            if i + 4 < B:
+                quantise_e(i + 4)
+            if i + 6 < B:
+                regroup_e_v(i + 6)
+
+        tp = psum.tile([P, 2, P], F32, name="bank")
         for nt in range(2):
             nc.tensor.transpose(tp[:, nt, :], rowmax[:, nt, :], ident[:])
         th = keep.tile([P, N], F32, name="th")

@@ -25,8 +25,6 @@ KP = 2
 def scalar_share(b):
     if b < 2:
         return 1024
-    if b < 4:
-        return 0
     return 512
 
 
@@ -112,13 +110,16 @@ def tile_parallelcoattention_t_kernel(tc, embedding, heatm, W_b, out):
                 in_=e_raw[b][:, c, :, n0:n1].rearrange("p t (g i) -> p g t i", i=4),
             )
 
+        def grouped_tile(b):
+            if b not in e_grouped:
+                e_grouped[b] = stage.tile([P, KP, N, PACK], BF16, name="eg", bufs=4, align_bytes=64)
+
         def regroup_e_s(b):
-            e_grouped[b] = stage.tile([P, KP, N, PACK], BF16, name="eg", bufs=4, align_bytes=64)
-            share = scalar_share(b)
-            if share > 0:
-                regroup_part(nc.scalar.copy, b, 1, N - share // PACK, N)
+            grouped_tile(b)
+            regroup_part(nc.scalar.copy, b, 1, N - scalar_share(b) // PACK, N)
 
         def regroup_e_v(b):
+            grouped_tile(b)
             share = scalar_share(b)
             regroup_part(nc.vector.tensor_copy, b, 0, 0, N)
             if share < 1024:
@@ -249,68 +250,69 @@ def tile_parallelcoattention_t_kernel(tc, embedding, heatm, W_b, out):
         quantise_e(1)
         regroup_w_v(1, 1)
         regroup_w_s(1, 1)
+        regroup_e_s(2)
         for b in range(2):
             for nh in range(2):
                 mm1(b, 0, nh, all_j)
                 evacuate(b, 0, nh)
         quantise_w(1, 0)
         quantise_w(1, 1)
-        regroup_e_s(2)
         regroup_e_v(2)
         quantise_w(1, 2)
         quantise_w(1, 3)
         quantise_e(2)
-        regroup_e_s(3)
         regroup_e_v(3)
-        regroup_e_s(4)
         regroup_e_v(4)
         for j in all_j:
             for b in range(2):
                 for nh in range(2):
                     mm1(b, 1, nh, [j])
-        for b in range(2):
-            for nh in range(2):
-                evacuate(b, 1, nh)
+        evacuate(0, 1, 0)
+        evacuate(0, 1, 1)
+        regroup_e_s(3)
+        evacuate(1, 1, 0)
+        evacuate(1, 1, 1)
         quantise_t(0)
         quantise_e(3)
-        quantise_t(1)
-        regroup_e_s(5)
         regroup_e_v(5)
 
         for i in range(B):
-            if i + 6 < B:
-                regroup_e_s(i + 6)
-            if i + 2 < B - 1:
-                for co in range(KP):
-                    for nh in range(2):
-                        mm1(i + 2, co, nh, all_j)
-                        evacuate(i + 2, co, nh)
-            if i + 2 == B - 1:
-                for nh in range(2):
-                    for co in range(KP):
-                        mm1(i + 2, co, nh, all_j)
-                        evacuate(i + 2, co, nh)
+            if i + 2 < B:
+                for x in range(4):
+                    if i + 2 == B - 1:
+                        co, nh = x % 2, x // 2
+                    else:
+                        co, nh = x // 2, x % 2
+                    mm1(i + 2, co, nh, all_j)
+                    evacuate(i + 2, co, nh)
+                    if x == 0 and i + 4 < B:
+                        regroup_e_s(i + 4)
             mm2(i)
+            if i + 1 < B - 1:
+                quantise_t(i + 1)
             if i + 2 == B - 1:
                 quantise_t_half(B - 1, 0)
-                row_max(i)
+            row_max(i)
+            if i + 2 == B - 1:
                 quantise_t_half(B - 1, 1)
-            else:
-                row_max(i)
-                if i + 2 < B:
-                    quantise_t(i + 2)
             if i + 4 < B:
                 quantise_e(i + 4)
             if i + 6 < B:
                 regroup_e_v(i + 6)
 
-        tp = psum.tile([P, 2, P], F32, name="bank")
-        for nt in range(2):
-            nc.tensor.transpose(tp[:, nt, :], rowmax[:, nt, :], ident[:])
+        tp_max = psum.tile([P, 2, P], F32, name="bank")
+        tp_tanh = psum.tile([P, 2, P], F32, name="bank")
+        for tp in (tp_max, tp_tanh):
+            for nt in range(2):
+                nc.tensor.transpose(tp[:, nt, :], rowmax[:, nt, :], ident[:])
+        negx = keep.tile([P, 1], F32, name="negx")
+        nc.vector.tensor_reduce(
+            out=negx[:], in_=tp_max[:].rearrange("p t n -> p (t n)"), axis=AX.X, op=ALU.max, negate=True
+        )
         th = keep.tile([P, N], F32, name="th")
-        nc.scalar.activation(out=th[:], in_=tp[:].rearrange("p t n -> p (t n)"), func=ACT.Tanh)
+        nc.scalar.activation(out=th[:], in_=tp_tanh[:].rearrange("p t n -> p (t n)"), func=ACT.Tanh)
         negmax = keep.tile([P, 1], F32, name="negmax")
-        nc.vector.tensor_reduce(out=negmax[:], in_=th[:], axis=AX.X, op=ALU.max, negate=True)
+        nc.scalar.activation(out=negmax[:], in_=negx[:], func=ACT.Tanh)
         ex = keep.tile([P, N], F32, name="ex")
         esum = keep.tile([P, 1], F32, name="esum")
         nc.scalar.activation(

@@ -22,6 +22,12 @@ N = 256
 KP = 2
 
 
+SHIFT_E_CODES = 0
+SHIFT_E_SCALES = 0
+SHIFT_L_CODES = 64
+SHIFT_L_SCALES = 0
+
+
 def scalar_share(b):
     if b < 2:
         return 1024
@@ -35,6 +41,10 @@ def tile_parallelcoattention_t_kernel(tc, embedding, heatm, W_b, out):
         stage = ctx.enter_context(tc.tile_pool(name="stage", bufs=3))
         psum = ctx.enter_context(tc.psum_pool(name="psum", bufs=8))
         ctx.enter_context(tc.manual_schedule())
+
+        def placed(pool, name, dtype, size, width, shift):
+            t = pool.tile([P, shift // size + width], dtype, name=name, align_bytes=256)
+            return t[:, shift // size : shift // size + width]
 
         warm = keep.tile([P, 1], F32, name="warm")
         nc.vector.memset(warm[:], 0.0)
@@ -90,15 +100,15 @@ def tile_parallelcoattention_t_kernel(tc, embedding, heatm, W_b, out):
             regroup_w(nc.scalar.copy, ck, co, 1)
 
         def quantise_w(co, j):
-            c = keep.tile([P, KP, P], U32, name="wc%d%d" % (co, j), align_bytes=64)
-            s = keep.tile([P, KP, P], U8, name="ws%d%d" % (co, j), align_bytes=64)
+            c = placed(keep, "wc%d%d" % (co, j), U32, 4, KP * P, SHIFT_L_CODES)
+            s = placed(keep, "ws%d%d" % (co, j), U8, 1, KP * P, SHIFT_L_SCALES)
             nc.vector.quantize_mx(
-                out=c[:].rearrange("p c q -> p (c q)").bitcast(FP8X4),
-                scales=s[:].rearrange("p c q -> p (c q)"),
+                out=c.bitcast(FP8X4),
+                scales=s,
                 in_=w_grouped[(co, j // 2)][:, j % 2, :, :, :].rearrange("p c q k -> p (c q k)"),
             )
-            w_codes[(co, j)] = c
-            w_scales[(co, j)] = s
+            w_codes[(co, j)] = c.rearrange("p (c q) -> p c q", c=KP)
+            w_scales[(co, j)] = s.rearrange("p (c q) -> p c q", c=KP)
 
         e_grouped = {}
         e_codes = {}
@@ -126,15 +136,15 @@ def tile_parallelcoattention_t_kernel(tc, embedding, heatm, W_b, out):
                 regroup_part(nc.vector.tensor_copy, b, 1, 0, N - share // PACK)
 
         def quantise_e(b):
-            c = keep.tile([P, KP, N], U32, name="ec%d" % b, align_bytes=64)
-            s = keep.tile([P, KP, N], U8, name="es%d" % b, align_bytes=64)
+            c = placed(keep, "ec%d" % b, U32, 4, KP * N, SHIFT_E_CODES)
+            s = placed(keep, "es%d" % b, U8, 1, KP * N, SHIFT_E_SCALES)
             nc.vector.quantize_mx(
-                out=c[:].rearrange("p c n -> p (c n)").bitcast(FP8X4),
-                scales=s[:].rearrange("p c n -> p (c n)"),
+                out=c.bitcast(FP8X4),
+                scales=s,
                 in_=e_grouped[b][:].rearrange("p c n k -> p (c n k)"),
             )
-            e_codes[b] = c
-            e_scales[b] = s
+            e_codes[b] = c.rearrange("p (c n) -> p c n", c=KP)
+            e_scales[b] = s.rearrange("p (c n) -> p c n", c=KP)
 
         t_banks = {}
         t_grouped = {}
@@ -172,27 +182,27 @@ def tile_parallelcoattention_t_kernel(tc, embedding, heatm, W_b, out):
             nc.scalar.copy(out=dst, in_=t_banks[(b, co, nh)][:].rearrange("p j n -> p n j"))
 
         def quantise_t(b):
-            c = stage.tile([P, 2, KP, P], U32, name="tc", align_bytes=64)
-            s = stage.tile([P, 2, KP, P], U8, name="ts", align_bytes=64)
+            c = placed(stage, "tc", U32, 4, 2 * KP * P, SHIFT_L_CODES)
+            s = placed(stage, "ts", U8, 1, 2 * KP * P, SHIFT_L_SCALES)
             nc.vector.quantize_mx(
-                out=c[:].rearrange("p h c n -> p (h c n)").bitcast(FP8X4),
-                scales=s[:].rearrange("p h c n -> p (h c n)"),
+                out=c.bitcast(FP8X4),
+                scales=s,
                 in_=t_grouped[b][:].rearrange("p h c n k -> p (h c n k)"),
             )
             for nh in range(2):
-                t_codes[(b, nh)] = c[:, nh, :, :]
-                t_scales[(b, nh)] = s[:, nh, :, :]
+                t_codes[(b, nh)] = c.rearrange("p (h c n) -> p h c n", h=2, c=KP)[:, nh, :, :]
+                t_scales[(b, nh)] = s.rearrange("p (h c n) -> p h c n", h=2, c=KP)[:, nh, :, :]
 
         def quantise_t_half(b, nh):
-            c = keep.tile([P, KP, P], U32, name="tcl%d" % nh, align_bytes=64)
-            s = keep.tile([P, KP, P], U8, name="tsl%d" % nh, align_bytes=64)
+            c = placed(keep, "tcl%d" % nh, U32, 4, KP * P, SHIFT_L_CODES)
+            s = placed(keep, "tsl%d" % nh, U8, 1, KP * P, SHIFT_L_SCALES)
             nc.vector.quantize_mx(
-                out=c[:].rearrange("p c n -> p (c n)").bitcast(FP8X4),
-                scales=s[:].rearrange("p c n -> p (c n)"),
+                out=c.bitcast(FP8X4),
+                scales=s,
                 in_=t_grouped[(b, nh)][:].rearrange("p c n k -> p (c n k)"),
             )
-            t_codes[(b, nh)] = c[:]
-            t_scales[(b, nh)] = s[:]
+            t_codes[(b, nh)] = c.rearrange("p (c n) -> p c n", c=KP)
+            t_scales[(b, nh)] = s.rearrange("p (c n) -> p c n", c=KP)
 
         c_banks = {}
 

@@ -22,6 +22,9 @@ N = 256
 KP = 2
 
 
+W_VECTOR = 80
+
+
 SHIFT_E_CODES = 0
 SHIFT_E_SCALES = 0
 SHIFT_L_CODES = 64
@@ -84,20 +87,19 @@ def tile_parallelcoattention_t_kernel(tc, embedding, heatm, W_b, out):
         w_codes = {}
         w_scales = {}
         for co in range(KP):
-            for jp in range(2):
-                w_grouped[(co, jp)] = keep.tile(
-                    [P, 2, KP, P, PACK], BF16, name="wg%d%d" % (co, jp), align_bytes=64
-                )
+            w_grouped[co] = keep.tile([P, PACK, KP, P, PACK], BF16, name="wg%d" % co, align_bytes=64)
 
-        def regroup_w(copy, ck, co, jp):
-            src = w_raw[(ck, co)][:].rearrange("p k (q j) -> p j q k", j=PACK)
-            copy(out=w_grouped[(co, jp)][:, :, ck, :, :], in_=src[:, 2 * jp : 2 * jp + 2, :, :])
+        def regroup_w(copy, ck, co, q0, q1):
+            copy(
+                out=w_grouped[co][:, :, ck, q0:q1, :].rearrange("p j q k -> p q k j"),
+                in_=w_raw[(ck, co)][:, :, PACK * q0 : PACK * q1].rearrange("p k (q j) -> p q k j", j=PACK),
+            )
 
         def regroup_w_v(ck, co):
-            regroup_w(nc.vector.tensor_copy, ck, co, 0)
+            regroup_w(nc.vector.tensor_copy, ck, co, 0, W_VECTOR)
 
         def regroup_w_s(ck, co):
-            regroup_w(nc.scalar.copy, ck, co, 1)
+            regroup_w(nc.scalar.copy, ck, co, W_VECTOR, P)
 
         def quantise_w(co, j):
             c = placed(keep, "wc%d%d" % (co, j), U32, 4, KP * P, SHIFT_L_CODES)
@@ -105,7 +107,7 @@ def tile_parallelcoattention_t_kernel(tc, embedding, heatm, W_b, out):
             nc.vector.quantize_mx(
                 out=c.bitcast(FP8X4),
                 scales=s,
-                in_=w_grouped[(co, j // 2)][:, j % 2, :, :, :].rearrange("p c q k -> p (c q k)"),
+                in_=w_grouped[co][:, j, :, :, :].rearrange("p c q k -> p (c q k)"),
             )
             w_codes[(co, j)] = c.rearrange("p (c q) -> p c q", c=KP)
             w_scales[(co, j)] = s.rearrange("p (c q) -> p c q", c=KP)

@@ -74,9 +74,9 @@ def tile_parallelcoattention_t_kernel(tc, embedding, heatm, W_b, out):
             )
             e_raw[b] = t
 
+        load_e(0)
         load_w(0, 0)
         load_w(1, 0)
-        load_e(0)
         load_e(1)
         load_w(0, 1)
         load_w(1, 1)
@@ -121,6 +121,10 @@ def tile_parallelcoattention_t_kernel(tc, embedding, heatm, W_b, out):
                 out=e_grouped[b][:, c, n0:n1, :].rearrange("p (g i) t -> p g t i", i=4),
                 in_=e_raw[b][:, c, :, n0:n1].rearrange("p t (g i) -> p g t i", i=4),
             )
+
+        def rg_e(copy, b, c, n0, n1):
+            grouped_tile(b)
+            regroup_part(copy, b, c, n0, n1)
 
         def grouped_tile(b):
             if b not in e_grouped:
@@ -244,41 +248,46 @@ def tile_parallelcoattention_t_kernel(tc, embedding, heatm, W_b, out):
                 )
 
         all_j = [0, 1, 2, 3]
-        regroup_w_v(0, 0)
-        regroup_w_s(0, 0)
-        regroup_w_v(1, 0)
-        regroup_w_s(1, 0)
-        quantise_w(0, 0)
-        quantise_w(0, 1)
-        regroup_e_s(0)
-        regroup_e_v(0)
-        quantise_w(0, 2)
-        quantise_w(0, 3)
-        regroup_e_s(1)
-        regroup_e_v(1)
+        rg_e(nc.scalar.copy, 0, 1, 128, 256)
+        rg_e(nc.vector.tensor_copy, 0, 0, 0, 256)
+        rg_e(nc.vector.tensor_copy, 0, 1, 0, 128)
+        regroup_w(nc.vector.tensor_copy, 0, 0, 0, 80)
+        regroup_w(nc.scalar.copy, 0, 0, 80, P)
         quantise_e(0)
-        regroup_w_v(0, 1)
-        regroup_w_s(0, 1)
+        regroup_w(nc.vector.tensor_copy, 1, 0, 0, 80)
+        regroup_w(nc.scalar.copy, 1, 0, 80, P)
+        rg_e(nc.scalar.copy, 1, 1, 0, 256)
+        for j in (0, 1):
+            quantise_w(0, j)
+            for nh in range(2):
+                mm1(0, 0, nh, [j])
+        rg_e(nc.vector.tensor_copy, 1, 0, 0, 256)
+        for j in (2, 3):
+            quantise_w(0, j)
+            for nh in range(2):
+                mm1(0, 0, nh, [j])
+        regroup_w(nc.vector.tensor_copy, 0, 1, 0, 64)
+        regroup_w(nc.scalar.copy, 0, 1, 64, P)
         quantise_e(1)
-        regroup_w_v(1, 1)
-        regroup_w_s(1, 1)
-        regroup_e_s(2)
+        for nh in range(2):
+            mm1(1, 0, nh, all_j)
+        regroup_w(nc.vector.tensor_copy, 1, 1, 0, 64)
+        regroup_w(nc.scalar.copy, 1, 1, 64, P)
+        rg_e(nc.scalar.copy, 2, 1, 0, 256)
         for b in range(2):
             for nh in range(2):
-                mm1(b, 0, nh, all_j)
                 evacuate(b, 0, nh)
         quantise_w(1, 0)
         quantise_w(1, 1)
-        regroup_e_v(2)
         quantise_w(1, 2)
+        rg_e(nc.vector.tensor_copy, 2, 0, 0, 256)
         quantise_w(1, 3)
-        quantise_e(2)
-        regroup_e_v(3)
-        regroup_e_v(4)
         for j in all_j:
             for b in range(2):
                 for nh in range(2):
                     mm1(b, 1, nh, [j])
+        quantise_e(2)
+        regroup_e_v(3)
         evacuate(0, 1, 0)
         evacuate(0, 1, 1)
         regroup_e_s(3)
@@ -286,7 +295,7 @@ def tile_parallelcoattention_t_kernel(tc, embedding, heatm, W_b, out):
         evacuate(1, 1, 1)
         quantise_t(0)
         quantise_e(3)
-        regroup_e_v(5)
+        regroup_e_v(4)
 
         for i in range(B):
             if i + 2 < B:
@@ -309,8 +318,8 @@ def tile_parallelcoattention_t_kernel(tc, embedding, heatm, W_b, out):
                 quantise_t_half(B - 1, 1)
             if i + 4 < B:
                 quantise_e(i + 4)
-            if i + 6 < B:
-                regroup_e_v(i + 6)
+            if i + 5 < B:
+                regroup_e_v(i + 5)
 
         tp_max = psum.tile([P, 2, P], F32, name="bank")
         tp_tanh = psum.tile([P, 2, P], F32, name="bank")

from contextlib import ExitStack

import concourse.mybir as mybir
from concourse.masks import make_identity

FLOPS = 2 * 4096 * 1024 * 1024 + 16 * 2 * 256 * 256 * 1024
BYTES = 16 * 1024 * 256 * 2 + 1024 * 1024 * 2 + 16 * 256 * 4

BF16 = mybir.dt.bfloat16
F32 = mybir.dt.float32
U32 = mybir.dt.uint32
U8 = mybir.dt.uint8
FP8X4 = mybir.dt.float8_e4m3fn_x4
ACT = mybir.ActivationFunctionType
ALU = mybir.AluOpType
AX = mybir.AxisListType

P = 128
PACK = 4
B = 16
N = 256
KP = 2


W_VECTOR = 80


SHIFT_E_CODES = 0
SHIFT_E_SCALES = 0
SHIFT_L_CODES = 64
SHIFT_L_SCALES = 0


def scalar_share(b):
    if b < 2:
        return 1024
    return 512


def tile_parallelcoattention_t_kernel(tc, embedding, heatm, W_b, out):
    nc = tc.nc
    with ExitStack() as ctx:
        keep = ctx.enter_context(tc.tile_pool(name="keep", bufs=1))
        stage = ctx.enter_context(tc.tile_pool(name="stage", bufs=3))
        psum = ctx.enter_context(tc.psum_pool(name="psum", bufs=8))
        ctx.enter_context(tc.manual_schedule())

        def placed(pool, name, dtype, size, width, shift):
            t = pool.tile([P, shift // size + width], dtype, name=name, align_bytes=256)
            return t[:, shift // size : shift // size + width]

        warm = keep.tile([P, 1], F32, name="warm")
        nc.vector.memset(warm[:], 0.0)
        warm2 = keep.tile([P, 1], F32, name="warm2")
        nc.scalar.activation(out=warm2[:], in_=warm[:], func=ACT.Tanh)
        rowmax = keep.tile([P, 2, P], F32, name="rowmax")
        nc.vector.memset(rowmax[:], 0.0)
        ident = keep.tile([P, P], F32, name="ident")
        make_identity(nc, ident[:])

        w_view = W_b.rearrange("(c p k) w -> c p k w", c=KP, p=P, k=PACK)
        w_raw = {}
        e_raw = {}

        def load_w(ck, co):
            t = keep.tile([P, PACK, 512], BF16, name="wraw%d%d" % (ck, co))
            nc.sync.dma_start(out=t[:], in_=w_view[ck][:, :, co * 512 : (co + 1) * 512])
            w_raw[(ck, co)] = t

        def load_e(b):
            t = keep.tile([P, KP, PACK, N], BF16, name="eraw%d" % b)
            nc.sync.dma_start(
                out=t[:], in_=embedding[b].rearrange("(c p k) n -> p c k n", c=KP, p=P, k=PACK)
            )
            e_raw[b] = t

        load_e(0)
        load_w(0, 0)
        load_w(1, 0)
        load_e(1)
        load_w(0, 1)
        load_w(1, 1)
        for b in range(2, B):
            load_e(b)

        w_grouped = {}
        w_codes = {}
        w_scales = {}
        for co in range(KP):
            w_grouped[co] = keep.tile([P, PACK, KP, P, PACK], BF16, name="wg%d" % co, align_bytes=64)

        def regroup_w(copy, ck, co, q0, q1):
            copy(
                out=w_grouped[co][:, :, ck, q0:q1, :].rearrange("p j q k -> p q k j"),
                in_=w_raw[(ck, co)][:, :, PACK * q0 : PACK * q1].rearrange("p k (q j) -> p q k j", j=PACK),
            )

        def regroup_w_v(ck, co):
            regroup_w(nc.vector.tensor_copy, ck, co, 0, W_VECTOR)

        def regroup_w_s(ck, co):
            regroup_w(nc.scalar.copy, ck, co, W_VECTOR, P)

        def quantise_w(co, j):
            c = placed(keep, "wc%d%d" % (co, j), U32, 4, KP * P, SHIFT_L_CODES)
            s = placed(keep, "ws%d%d" % (co, j), U8, 1, KP * P, SHIFT_L_SCALES)
            nc.vector.quantize_mx(
                out=c.bitcast(FP8X4),
                scales=s,
                in_=w_grouped[co][:, j, :, :, :].rearrange("p c q k -> p (c q k)"),
            )
            w_codes[(co, j)] = c.rearrange("p (c q) -> p c q", c=KP)
            w_scales[(co, j)] = s.rearrange("p (c q) -> p c q", c=KP)

        e_grouped = {}
        e_codes = {}
        e_scales = {}

        def regroup_part(copy, b, c, n0, n1):
            copy(
                out=e_grouped[b][:, c, n0:n1, :].rearrange("p (g i) t -> p g t i", i=4),
                in_=e_raw[b][:, c, :, n0:n1].rearrange("p t (g i) -> p g t i", i=4),
            )

        def rg_e(copy, b, c, n0, n1):
            grouped_tile(b)
            regroup_part(copy, b, c, n0, n1)

        def grouped_tile(b):
            if b not in e_grouped:
                e_grouped[b] = stage.tile([P, KP, N, PACK], BF16, name="eg", bufs=4, align_bytes=64)

        def regroup_e_s(b):
            grouped_tile(b)
            regroup_part(nc.scalar.copy, b, 1, N - scalar_share(b) // PACK, N)

        def regroup_e_v(b):
            grouped_tile(b)
            share = scalar_share(b)
            regroup_part(nc.vector.tensor_copy, b, 0, 0, N)
            if share < 1024:
                regroup_part(nc.vector.tensor_copy, b, 1, 0, N - share // PACK)

        def quantise_e(b):
            c = placed(keep, "ec%d" % b, U32, 4, KP * N, SHIFT_E_CODES)
            s = placed(keep, "es%d" % b, U8, 1, KP * N, SHIFT_E_SCALES)
            nc.vector.quantize_mx(
                out=c.bitcast(FP8X4),
                scales=s,
                in_=e_grouped[b][:].rearrange("p c n k -> p (c n k)"),
            )
            e_codes[b] = c.rearrange("p (c n) -> p c n", c=KP)
            e_scales[b] = s.rearrange("p (c n) -> p c n", c=KP)

        t_banks = {}
        t_grouped = {}
        t_codes = {}
        t_scales = {}

        def mm1(b, co, nh, js):
            if (b, co, nh) not in t_banks:
                t_banks[(b, co, nh)] = psum.tile([P, PACK, P], F32, name="bank")
            bank = t_banks[(b, co, nh)]
            cols = slice(nh * P, (nh + 1) * P)
            for j in js:
                for ck in range(KP):
                    nc.tensor.matmul_mx(
                        out=bank[:, j, :],
                        lhsT=w_codes[(co, j)][:, ck, :].bitcast(FP8X4),
                        lhsT_scale=w_scales[(co, j)][:, ck, :],
                        rhs=e_codes[b][:, ck, cols].bitcast(FP8X4),
                        rhs_scale=e_scales[b][:, ck, cols],
                        start=(ck == 0),
                        stop=(ck == KP - 1),
                    )

        def evacuate(b, co, nh):
            if b == B - 1:
                if (b, nh) not in t_grouped:
                    t_grouped[(b, nh)] = keep.tile(
                        [P, KP, P, PACK], BF16, name="tgl%d" % nh, align_bytes=64
                    )
                dst = t_grouped[(b, nh)][:, co, :, :]
            else:
                if b not in t_grouped:
                    t_grouped[b] = stage.tile([P, 2, KP, P, PACK], BF16, name="tg", align_bytes=64)
                dst = t_grouped[b][:, nh, co, :, :]
            nc.scalar.copy(out=dst, in_=t_banks[(b, co, nh)][:].rearrange("p j n -> p n j"))

        def quantise_t(b):
            c = placed(stage, "tc", U32, 4, 2 * KP * P, SHIFT_L_CODES)
            s = placed(stage, "ts", U8, 1, 2 * KP * P, SHIFT_L_SCALES)
            nc.vector.quantize_mx(
                out=c.bitcast(FP8X4),
                scales=s,
                in_=t_grouped[b][:].rearrange("p h c n k -> p (h c n k)"),
            )
            for nh in range(2):
                t_codes[(b, nh)] = c.rearrange("p (h c n) -> p h c n", h=2, c=KP)[:, nh, :, :]
                t_scales[(b, nh)] = s.rearrange("p (h c n) -> p h c n", h=2, c=KP)[:, nh, :, :]

        def quantise_t_half(b, nh):
            c = placed(keep, "tcl%d" % nh, U32, 4, KP * P, SHIFT_L_CODES)
            s = placed(keep, "tsl%d" % nh, U8, 1, KP * P, SHIFT_L_SCALES)
            nc.vector.quantize_mx(
                out=c.bitcast(FP8X4),
                scales=s,
                in_=t_grouped[(b, nh)][:].rearrange("p c n k -> p (c n k)"),
            )
            t_codes[(b, nh)] = c.rearrange("p (c n) -> p c n", c=KP)
            t_scales[(b, nh)] = s.rearrange("p (c n) -> p c n", c=KP)

        c_banks = {}

        def mm2_half(b, nt, dst):
            for c in range(KP):
                nc.tensor.matmul_mx(
                    out=dst,
                    lhsT=t_codes[(b, nt)][:, c, :].bitcast(FP8X4),
                    lhsT_scale=t_scales[(b, nt)][:, c, :],
                    rhs=e_codes[b][:, c, :].bitcast(FP8X4),
                    rhs_scale=e_scales[b][:, c, :],
                    start=(c == 0),
                    stop=(c == KP - 1),
                )

        def mm2(b):
            if b == B - 1:
                for nt in range(2):
                    bank = psum.tile([P, N], F32, name="bank")
                    mm2_half(b, nt, bank[:])
                    c_banks[(b, nt)] = bank
            else:
                bank = psum.tile([P, 2, N], F32, name="bank")
                for nt in range(2):
                    mm2_half(b, nt, bank[:, nt, :])
                c_banks[b] = bank

        def row_max(b):
            if b == B - 1:
                for nt in range(2):
                    nc.vector.tensor_reduce(
                        out=rowmax[:, nt, b : b + 1], in_=c_banks[(b, nt)][:], axis=AX.X, op=ALU.max
                    )
            else:
                nc.vector.tensor_reduce(
                    out=rowmax[:, :, b], in_=c_banks[b][:], axis=AX.X, op=ALU.max
                )

        all_j = [0, 1, 2, 3]
        rg_e(nc.scalar.copy, 0, 1, 128, 256)
        rg_e(nc.vector.tensor_copy, 0, 0, 0, 256)
        rg_e(nc.vector.tensor_copy, 0, 1, 0, 128)
        regroup_w(nc.vector.tensor_copy, 0, 0, 0, 80)
        regroup_w(nc.scalar.copy, 0, 0, 80, P)
        quantise_e(0)
        regroup_w(nc.vector.tensor_copy, 1, 0, 0, 80)
        regroup_w(nc.scalar.copy, 1, 0, 80, P)
        rg_e(nc.scalar.copy, 1, 1, 0, 256)
        for j in (0, 1):
            quantise_w(0, j)
            for nh in range(2):
                mm1(0, 0, nh, [j])
        rg_e(nc.vector.tensor_copy, 1, 0, 0, 256)
        for j in (2, 3):
            quantise_w(0, j)
            for nh in range(2):
                mm1(0, 0, nh, [j])
        regroup_w(nc.vector.tensor_copy, 0, 1, 0, 64)
        regroup_w(nc.scalar.copy, 0, 1, 64, P)
        quantise_e(1)
        for nh in range(2):
            mm1(1, 0, nh, all_j)
        regroup_w(nc.vector.tensor_copy, 1, 1, 0, 64)
        regroup_w(nc.scalar.copy, 1, 1, 64, P)
        rg_e(nc.scalar.copy, 2, 1, 0, 256)
        for b in range(2):
            for nh in range(2):
                evacuate(b, 0, nh)
        quantise_w(1, 0)
        quantise_w(1, 1)
        quantise_w(1, 2)
        rg_e(nc.vector.tensor_copy, 2, 0, 0, 256)
        quantise_w(1, 3)
        for j in all_j:
            for b in range(2):
                for nh in range(2):
                    mm1(b, 1, nh, [j])
        quantise_e(2)
        regroup_e_v(3)
        evacuate(0, 1, 0)
        evacuate(0, 1, 1)
        regroup_e_s(3)
        evacuate(1, 1, 0)
        evacuate(1, 1, 1)
        quantise_t(0)
        quantise_e(3)
        regroup_e_v(4)

        for i in range(B):
            if i + 2 < B:
                for x in range(4):
                    if i + 2 == B - 1:
                        co, nh = x % 2, x // 2
                    else:
                        co, nh = x // 2, x % 2
                    mm1(i + 2, co, nh, all_j)
                    evacuate(i + 2, co, nh)
                    if x == 0 and i + 4 < B:
                        regroup_e_s(i + 4)
            mm2(i)
            if i + 1 < B - 1:
                quantise_t(i + 1)
            if i + 2 == B - 1:
                quantise_t_half(B - 1, 0)
            row_max(i)
            if i + 2 == B - 1:
                quantise_t_half(B - 1, 1)
            if i + 4 < B:
                quantise_e(i + 4)
            if i + 5 < B:
                regroup_e_v(i + 5)

        tp_max = psum.tile([P, 2, P], F32, name="bank")
        tp_tanh = psum.tile([P, 2, P], F32, name="bank")
        for tp in (tp_max, tp_tanh):
            for nt in range(2):
                nc.tensor.transpose(tp[:, nt, :], rowmax[:, nt, :], ident[:])
        negx = keep.tile([P, 1], F32, name="negx")
        nc.vector.tensor_reduce(
            out=negx[:], in_=tp_max[:].rearrange("p t n -> p (t n)"), axis=AX.X, op=ALU.max, negate=True
        )
        th = keep.tile([P, N], F32, name="th")
        nc.scalar.activation(out=th[:], in_=tp_tanh[:].rearrange("p t n -> p (t n)"), func=ACT.Tanh)
        negmax = keep.tile([P, 1], F32, name="negmax")
        nc.scalar.activation(out=negmax[:], in_=negx[:], func=ACT.Tanh)
        ex = keep.tile([P, N], F32, name="ex")
        esum = keep.tile([P, 1], F32, name="esum")
        nc.scalar.activation(
            out=ex[:], in_=th[:], func=ACT.Exp, bias=negmax[:, 0:1], scale=1.0, accum_out=esum[:]
        )
        rsum = keep.tile([P, 1], F32, name="rsum")
        nc.vector.reciprocal(out=rsum[:], in_=esum[:])
        res = keep.tile([P, N], F32, name="res")
        nc.vector.tensor_scalar_mul(out=res[:], in0=ex[:], scalar1=rsum[:, 0:1])
        nc.sync.dma_start(out=out.rearrange("b n o -> b (n o)"), in_=res[0:B, :])
